import numpy as np
import ml_dtypes


def mxq(x, axis, fmt="e4m3"):
    dtype, down = {"e4m3": (ml_dtypes.float8_e4m3fn, 7), "e5m2": (ml_dtypes.float8_e5m2, 14)}[fmt]
    v = np.moveaxis(np.asarray(x, np.float32).astype(ml_dtypes.bfloat16).astype(np.float64), axis, -1)
    blocks = v.reshape(v.shape[:-1] + (-1, 32))
    amax = np.abs(blocks).max(-1, keepdims=True)
    byte = np.maximum(np.where(amax > 0, np.frexp(amax)[1] - 1 + 127, 0) - down, 1)
    scale = np.exp2(byte - 127.0)
    codes = (blocks / scale).astype(np.float32).astype(dtype).astype(np.float64)
    return np.moveaxis((codes * scale).reshape(v.shape), -1, axis)


WIDE = False


def mx_kscale(k):
    if not WIDE:
        return np.ones(k)
    levels = np.array([10, -10, 5, -5, 0])
    a = np.random.permutation(np.resize(levels, k // 512 * 4)).reshape(k // 512, 4)
    idx = np.arange(k)
    return np.exp2(a[idx // 512, idx % 128 // 32])


BF16 = ml_dtypes.bfloat16


def bf(x):
    return np.asarray(x, np.float32).astype(BF16)


def f64(x):
    return np.asarray(x).astype(np.float64)


B, S, D = 1, 1024, 512
SCALE = 1.0 / np.sqrt(D)


def setup_inputs():
    s = mx_kscale(D)
    return {"x1": bf(np.random.standard_normal((B, S, D)) * 2.0 * s), "x2": bf(np.random.standard_normal((B, S, D)) / s)}


def reference(x1, x2):
    x2 = f64(x2)
    scores = (mxq(f64(x1), 2, "e4m3") @ mxq(x2, 2, "e4m3").transpose(0, 2, 1)) * SCALE
    e = np.exp(scores - scores.max(-1, keepdims=True))
    return (mxq(e, 2, "e4m3") @ mxq(x2, 1, "e4m3")) / e.sum(-1, keepdims=True)

@@ -1,0 +1,284 @@
+import math
+from contextlib import ExitStack
+
+import concourse.mybir as mybir
+from concourse.masks import make_identity
+
+F32 = mybir.dt.float32
+BF16 = mybir.dt.bfloat16
+U32 = mybir.dt.uint32
+U8 = mybir.dt.uint8
+FP8X4 = mybir.dt.float8_e4m3fn_x4
+ACT = mybir.ActivationFunctionType
+ALU = mybir.AluOpType
+AX = mybir.AxisListType
+
+P = 128
+S_LEN = 1024
+D = 512
+NT = S_LEN // P
+SCALE = 1.0 / math.sqrt(D)
+FLOPS = 2 * 2 * S_LEN * S_LEN * D
+
+
+def tile_model_kernel(tc, x1, x2, out):
+    nc = tc.nc
+    with ExitStack() as ctx:
+        keep = ctx.enter_context(tc.tile_pool(name="keep", bufs=1))
+        psum = ctx.enter_context(tc.psum_pool(name="psum", bufs=8))
+        ctx.enter_context(tc.manual_schedule())
+
+        x2v = x2.flatten_outer_dims().rearrange("(g p j) d -> p g (j d)", g=2, p=P, j=4)
+        x1v = x1.flatten_outer_dims().rearrange("(p i) d -> p (i d)", i=NT)
+        outv = out.flatten_outer_dims().rearrange("(p i) d -> p i d", i=NT)
+
+        ident_f = keep.tile([P, P], F32, name="ident_f")
+        ident_b = keep.tile([P, P], BF16, name="ident_b")
+        warm = keep.tile([P, 1], F32, name="warm")
+        warm2 = keep.tile([P, 1], F32, name="warm2")
+
+        x2_sb = [keep.tile([P, 4 * D], BF16, name="x2_sb%d" % g) for g in range(2)]
+        x1_sb = [keep.tile([P, 2 * D], BF16, name="x1_sb%d" % c) for c in range(4)]
+        x2t_g = [keep.tile([P, 2048], BF16, name="x2t_g%d" % g, align_bytes=64) for g in range(2)]
+        x2t_c = [keep.tile([P, 512], U32, name="x2t_c%d" % g, align_bytes=64) for g in range(2)]
+        x2t_s = [keep.tile([P, 512], U8, name="x2t_s%d" % g, align_bytes=64) for g in range(2)]
+        x1t_g = [keep.tile([P, 1024], BF16, name="x1t_g%d" % c, align_bytes=64) for c in range(4)]
+        x1t_c = [keep.tile([P, 256], U32, name="x1t_c%d" % c, align_bytes=64) for c in range(4)]
+        x1t_s = [keep.tile([P, 256], U8, name="x1t_s%d" % c, align_bytes=64) for c in range(4)]
+        x2k_g = [keep.tile([P, 2048], BF16, name="x2k_g%d" % g, align_bytes=64) for g in range(2)]
+        x2k_c = [keep.tile([P, 512], U32, name="x2k_c%d" % g, align_bytes=64) for g in range(2)]
+        x2k_s = [keep.tile([P, 512], U8, name="x2k_s%d" % g, align_bytes=64) for g in range(2)]
+        e_sb = [keep.tile([P, S_LEN], BF16, name="e_sb%d" % i) for i in range(NT)]
+        e_g = [keep.tile([P, S_LEN], BF16, name="e_g%d" % i, align_bytes=64) for i in range(NT)]
+        e_c = [keep.tile([P, 256], U32, name="e_c%d" % i, align_bytes=64) for i in range(NT)]
+        e_s = [keep.tile([P, 256], U8, name="e_s%d" % i, align_bytes=64) for i in range(NT)]
+        o_sb = [keep.tile([P, D], F32, name="o_sb%d" % i) for i in range(NT)]
+        mx = [keep.tile([P, 2], F32, name="mx%d" % i) for i in range(NT)]
+        nb = [keep.tile([P, 1], F32, name="nb%d" % i) for i in range(NT)]
+        rs = [keep.tile([P, 2], F32, name="rs%d" % i) for i in range(NT)]
+        rt = [keep.tile([P, 1], F32, name="rt%d" % i) for i in range(NT)]
+        ri = [keep.tile([P, 1], F32, name="ri%d" % i) for i in range(NT)]
+
+        banks = {}
+
+        def copy_on(eng, dst, src):
+            if eng == "V":
+                nc.vector.tensor_copy(out=dst, in_=src)
+            else:
+                nc.scalar.copy(out=dst, in_=src)
+
+        def transpose_words(key, src_words):
+            xt = psum.tile([P, 512], F32, name="xt_" + key, tag="bank")
+            for s in range(4):
+                nc.tensor.transpose(xt[:, P * s:P * (s + 1)], src_words[:, P * s:P * (s + 1)], ident_f[:])
+            banks[key] = xt
+
+        def evacuate_words(key, dst_bf16, eng):
+            xt = banks[key]
+            copy_on(
+                eng,
+                dst_bf16.bitcast(F32).rearrange("p (t r u) -> p t r u", t=2, u=2),
+                xt[:].rearrange("p (t u r) -> p t r u", t=2, u=2),
+            )
+
+        def PX2(g, b):
+            transpose_words("x2_%d_%d" % (g, b), x2_sb[g][:].bitcast(F32)[:, 512 * b:512 * (b + 1)])
+
+        def EX2(g, b, eng):
+            evacuate_words("x2_%d_%d" % (g, b), x2t_g[g][:, 1024 * b:1024 * (b + 1)], eng)
+
+        def QX2(g):
+            nc.vector.quantize_mx(out=x2t_c[g][:].bitcast(FP8X4), scales=x2t_s[g][:], in_=x2t_g[g][:])
+
+        def PX1(c):
+            transpose_words("x1_%d" % c, x1_sb[c][:].bitcast(F32))
+
+        def EX1(c, eng):
+            evacuate_words("x1_%d" % c, x1t_g[c][:], eng)
+
+        def QX1(c):
+            nc.vector.quantize_mx(out=x1t_c[c][:].bitcast(FP8X4), scales=x1t_s[c][:], in_=x1t_g[c][:])
+
+        def R(g, h, eng):
+            dst = x2k_g[g][:, 1024 * h:1024 * (h + 1)].rearrange("p (c i t) -> p c t i", i=4, t=4)
+            src = x2_sb[g][:].rearrange("p (t d) -> p t d", t=4)[:, :, 256 * h:256 * (h + 1)]
+            copy_on(eng, dst, src.rearrange("p t (c i) -> p c t i", i=4))
+
+        def QK(g):
+            nc.vector.quantize_mx(out=x2k_c[g][:].bitcast(FP8X4), scales=x2k_s[g][:], in_=x2k_g[g][:])
+
+        def A(i, h):
+            sp = psum.tile([P, 512], F32, name="s_%d_%d" % (i, h), tag="bank")
+            c, t = i // 2, i % 2
+            nc.tensor.matmul_mx(
+                out=sp[:],
+                lhsT=x1t_c[c][:, P * t:P * (t + 1)].bitcast(FP8X4),
+                lhsT_scale=x1t_s[c][:, P * t:P * (t + 1)],
+                rhs=x2t_c[h][:].bitcast(FP8X4),
+                rhs_scale=x2t_s[h][:],
+                start=True,
+                stop=True,
+            )
+            banks["s_%d_%d" % (i, h)] = sp
+
+        def B(i):
+            for h in range(2):
+                nc.vector.tensor_reduce(out=mx[i][:, h:h + 1], in_=banks["s_%d_%d" % (i, h)][:], axis=AX.X, op=ALU.max)
+            nc.vector.tensor_scalar(
+                out=nb[i][:], in0=mx[i][:, 0:1], scalar1=mx[i][:, 1:2], scalar2=-SCALE, op0=ALU.max, op1=ALU.mult
+            )
+
+        def C(i):
+            for h in range(2):
+                nc.scalar.activation(
+                    out=e_sb[i][:, 512 * h:512 * (h + 1)],
+                    in_=banks["s_%d_%d" % (i, h)][:],
+                    func=ACT.Exp,
+                    bias=nb[i][:],
+                    scale=SCALE,
+                    accum_out=rs[i][:, h:h + 1],
+                )
+
+        def Dh(i, g, et, col):
+            for j in range(4):
+                k0 = 512 * g + P * j
+                nc.tensor.transpose(et[:, col + P * j:col + P * (j + 1)], e_sb[i][:, k0:k0 + P], ident_b[:])
+
+        def Dfull(i):
+            et = psum.tile([P, 1024], BF16, name="et_%d" % i, tag="bank")
+            Dh(i, 0, et, 0)
+            Dh(i, 1, et, 512)
+            banks["et_%d" % i] = et
+
+        def Efull(i, eng):
+            copy_on(
+                eng,
+                e_g[i][:].rearrange("p (g q j) -> p g q j", g=2, j=4),
+                banks["et_%d" % i][:].rearrange("p (g j q) -> p g q j", g=2, j=4),
+            )
+
+        def Dhalf(i, g):
+            et = psum.tile([P, 512], BF16, name="et_%d_%d" % (i, g), tag="bank")
+            Dh(i, g, et, 0)
+            banks["et_%d_%d" % (i, g)] = et
+
+        def Ehalf(i, g, eng):
+            copy_on(
+                eng,
+                e_g[i][:, 512 * g:512 * (g + 1)].rearrange("p (q j) -> p q j", j=4),
+                banks["et_%d_%d" % (i, g)][:].rearrange("p (j q) -> p q j", j=4),
+            )
+
+        def F(i):
+            nc.vector.quantize_mx(out=e_c[i][:].bitcast(FP8X4), scales=e_s[i][:], in_=e_g[i][:])
+
+        def G(i, c0, width):
+            op = psum.tile([P, width], F32, name="o_%d_%d" % (i, c0), tag="bank")
+            for g in range(2):
+                nc.tensor.matmul_mx(
+                    out=op[:],
+                    lhsT=e_c[i][:, P * g:P * (g + 1)].bitcast(FP8X4),
+                    lhsT_scale=e_s[i][:, P * g:P * (g + 1)],
+                    rhs=x2k_c[g][:, c0:c0 + width].bitcast(FP8X4),
+                    rhs_scale=x2k_s[g][:, c0:c0 + width],
+                    start=(g == 0),
+                    stop=(g == 1),
+                )
+            banks["o_%d_%d" % (i, c0)] = op
+
+        def Hs(i):
+            nc.vector.tensor_tensor(out=rt[i][:], in0=rs[i][:, 0:1], in1=rs[i][:, 1:2], op=ALU.add)
+            nc.vector.reciprocal(out=ri[i][:], in_=rt[i][:])
+
+        def H(i, c0, width, eng):
+            op = banks["o_%d_%d" % (i, c0)]
+            dst = o_sb[i][:, c0:c0 + width]
+            if eng == "V":
+                nc.vector.tensor_scalar(out=dst, in0=op[:], scalar1=ri[i][:], scalar2=None, op0=ALU.mult)
+            else:
+                nc.scalar.activation(out=dst, in_=op[:], func=ACT.Copy, scale=ri[i][:])
+            nc.sync.dma_start(out=outv[:, i, c0:c0 + width], in_=dst)
+
+        nc.vector.memset(warm[:], 0.0)
+        nc.scalar.activation(out=warm2[:], in_=warm[:], func=ACT.Exp)
+        make_identity(nc, ident_f[:])
+        make_identity(nc, ident_b[:])
+
+        for b in range(2):
+            nc.sync.dma_start(out=x2_sb[0][:, 1024 * b:1024 * (b + 1)], in_=x2v[:, 0, 1024 * b:1024 * (b + 1)])
+        nc.sync.dma_start(out=x1_sb[0][:], in_=x1v[:, 0:1024])
+        for b in range(2):
+            nc.sync.dma_start(out=x2_sb[1][:, 1024 * b:1024 * (b + 1)], in_=x2v[:, 1, 1024 * b:1024 * (b + 1)])
+        for c in range(1, 4):
+            nc.sync.dma_start(out=x1_sb[c][:], in_=x1v[:, 1024 * c:1024 * (c + 1)])
+
+        PX2(0, 0)
+        PX2(0, 1)
+        EX2(0, 0, "V")
+        EX2(0, 1, "S")
+        PX1(0)
+        EX1(0, "S")
+        QX2(0)
+        QX1(0)
+        PX2(1, 0)
+        PX2(1, 1)
+        EX2(1, 0, "S")
+        EX2(1, 1, "V")
+        PX1(1)
+        PX1(2)
+        A(0, 0)
+        A(1, 0)
+        QX2(1)
+        EX1(1, "S")
+        EX1(2, "S")
+        A(0, 1)
+        A(1, 1)
+        PX1(3)
+        R(0, 0, "S")
+        B(0)
+        for n in range(NT + 2):
+            if n < NT:
+                C(n)
+            if 0 <= n - 1 < NT - 1:
+                Dfull(n - 1)
+            if n - 1 == NT - 1:
+                Dhalf(n - 1, 0)
+                Dhalf(n - 1, 1)
+            if 0 <= n - 2:
+                F(n - 2)
+            if n + 1 < NT:
+                B(n + 1)
+            if n == 0:
+                QX1(1)
+                R(0, 1, "V")
+                QK(0)
+                EX1(3, "S")
+            if n == 1:
+                R(1, 0, "V")
+                R(1, 1, "V")
+                QK(1)
+                QX1(2)
+            if n == 2:
+                QX1(3)
+            if n + 2 < NT:
+                A(n + 2, 0)
+                A(n + 2, 1)
+            if 0 <= n - 2 < NT - 1:
+                G(n - 2, 0, 512)
+            if n - 2 == NT - 1:
+                G(n - 2, 0, 256)
+                G(n - 2, 256, 256)
+            if 0 <= n - 1 < NT - 2:
+                Efull(n - 1, "S")
+            if n - 1 == NT - 2:
+                Efull(n - 1, "V")
+            if n - 1 == NT - 1:
+                Ehalf(n - 1, 0, "S")
+                Ehalf(n - 1, 1, "V")
+            if 0 <= n - 2:
+                Hs(n - 2)
+            if 0 <= n - 2 < NT - 1:
+                H(n - 2, 0, 512, "S" if n - 2 >= 5 else "V")
+            if n - 2 == NT - 1:
+                H(n - 2, 0, 256, "V")
+                H(n - 2, 256, 256, "S")

@@ -11,21 +11,20 @@ U8 = mybir.dt.uint8
 FP8X4 = mybir.dt.float8_e4m3fn_x4
 ACT = mybir.ActivationFunctionType
 ALU = mybir.AluOpType
-AX = mybir.AxisListType
 
 P = 128
 S_LEN = 1024
-D = 512
+D_LEN = 512
 NT = S_LEN // P
-SCALE = 1.0 / math.sqrt(D)
-FLOPS = 2 * 2 * S_LEN * S_LEN * D
+SCALE = 1.0 / math.sqrt(D_LEN)
+FLOPS = 2 * 2 * S_LEN * S_LEN * D_LEN
 
 
 def tile_model_kernel(tc, x1, x2, out):
     nc = tc.nc
     with ExitStack() as ctx:
         keep = ctx.enter_context(tc.tile_pool(name="keep", bufs=1))
-        psum = ctx.enter_context(tc.psum_pool(name="psum", bufs=8))
+        psum = ctx.enter_context(tc.psum_pool(name="psum", bufs=1))
         ctx.enter_context(tc.manual_schedule())
 
         x2v = x2.flatten_outer_dims().rearrange("(g p j) d -> p g (j d)", g=2, p=P, j=4)
@@ -37,8 +36,8 @@ def tile_model_kernel(tc, x1, x2, out):
         warm = keep.tile([P, 1], F32, name="warm")
         warm2 = keep.tile([P, 1], F32, name="warm2")
 
-        x2_sb = [keep.tile([P, 4 * D], BF16, name="x2_sb%d" % g) for g in range(2)]
-        x1_sb = [keep.tile([P, 2 * D], BF16, name="x1_sb%d" % c) for c in range(4)]
+        x2_sb = [keep.tile([P, 4 * D_LEN], BF16, name="x2_sb%d" % g) for g in range(2)]
+        x1_sb = [keep.tile([P, 2 * D_LEN], BF16, name="x1_sb%d" % c) for c in range(4)]
         x2t_g = [keep.tile([P, 2048], BF16, name="x2t_g%d" % g, align_bytes=64) for g in range(2)]
         x2t_c = [keep.tile([P, 512], U32, name="x2t_c%d" % g, align_bytes=64) for g in range(2)]
         x2t_s = [keep.tile([P, 512], U8, name="x2t_s%d" % g, align_bytes=64) for g in range(2)]
@@ -48,41 +47,46 @@ def tile_model_kernel(tc, x1, x2, out):
         x2k_g = [keep.tile([P, 2048], BF16, name="x2k_g%d" % g, align_bytes=64) for g in range(2)]
         x2k_c = [keep.tile([P, 512], U32, name="x2k_c%d" % g, align_bytes=64) for g in range(2)]
         x2k_s = [keep.tile([P, 512], U8, name="x2k_s%d" % g, align_bytes=64) for g in range(2)]
+        sc = [keep.tile([P, S_LEN], F32, name="sc%d" % i) for i in range(NT)]
         e_sb = [keep.tile([P, S_LEN], BF16, name="e_sb%d" % i) for i in range(NT)]
         e_g = [keep.tile([P, S_LEN], BF16, name="e_g%d" % i, align_bytes=64) for i in range(NT)]
         e_c = [keep.tile([P, 256], U32, name="e_c%d" % i, align_bytes=64) for i in range(NT)]
         e_s = [keep.tile([P, 256], U8, name="e_s%d" % i, align_bytes=64) for i in range(NT)]
-        o_sb = [keep.tile([P, D], F32, name="o_sb%d" % i) for i in range(NT)]
-        mx = [keep.tile([P, 2], F32, name="mx%d" % i) for i in range(NT)]
+        o_sb = [keep.tile([P, D_LEN], F32, name="o_sb%d" % i) for i in range(NT)]
+        t0 = [keep.tile([P, 1], F32, name="t0_%d" % i) for i in range(NT)]
         nb = [keep.tile([P, 1], F32, name="nb%d" % i) for i in range(NT)]
-        rs = [keep.tile([P, 2], F32, name="rs%d" % i) for i in range(NT)]
-        rt = [keep.tile([P, 1], F32, name="rt%d" % i) for i in range(NT)]
+        rs = [keep.tile([P, 1], F32, name="rs%d" % i) for i in range(NT)]
         ri = [keep.tile([P, 1], F32, name="ri%d" % i) for i in range(NT)]
 
         banks = {}
 
+        def bank_tile(key, shape, dtype, bank):
+            t = psum.tile(shape, dtype, name="ps_" + key, tag="bank%d" % bank)
+            banks[key] = t
+            return t
+
         def copy_on(eng, dst, src):
             if eng == "V":
                 nc.vector.tensor_copy(out=dst, in_=src)
-            else:
+            elif eng == "S":
                 nc.scalar.copy(out=dst, in_=src)
+            else:
+                nc.gpsimd.tensor_scalar(out=dst, in0=src, scalar1=1.0, scalar2=0.0, op0=ALU.mult, op1=ALU.add)
 
-        def transpose_words(key, src_words):
-            xt = psum.tile([P, 512], F32, name="xt_" + key, tag="bank")
+        def transpose_words(key, src_words, bank):
+            xt = bank_tile(key, [P, 512], F32, bank)
             for s in range(4):
                 nc.tensor.transpose(xt[:, P * s:P * (s + 1)], src_words[:, P * s:P * (s + 1)], ident_f[:])
-            banks[key] = xt
 
         def evacuate_words(key, dst_bf16, eng):
-            xt = banks[key]
             copy_on(
                 eng,
                 dst_bf16.bitcast(F32).rearrange("p (t r u) -> p t r u", t=2, u=2),
-                xt[:].rearrange("p (t u r) -> p t r u", t=2, u=2),
+                banks[key][:].rearrange("p (t u r) -> p t r u", t=2, u=2),
             )
 
-        def PX2(g, b):
-            transpose_words("x2_%d_%d" % (g, b), x2_sb[g][:].bitcast(F32)[:, 512 * b:512 * (b + 1)])
+        def PX2(g, b, bank):
+            transpose_words("x2_%d_%d" % (g, b), x2_sb[g][:].bitcast(F32)[:, 512 * b:512 * (b + 1)], bank)
 
         def EX2(g, b, eng):
             evacuate_words("x2_%d_%d" % (g, b), x2t_g[g][:, 1024 * b:1024 * (b + 1)], eng)
@@ -90,8 +94,8 @@ def tile_model_kernel(tc, x1, x2, out):
         def QX2(g):
             nc.vector.quantize_mx(out=x2t_c[g][:].bitcast(FP8X4), scales=x2t_s[g][:], in_=x2t_g[g][:])
 
-        def PX1(c):
-            transpose_words("x1_%d" % c, x1_sb[c][:].bitcast(F32))
+        def PX1(c, bank):
+            transpose_words("x1_%d" % c, x1_sb[c][:].bitcast(F32), bank)
 
         def EX1(c, eng):
             evacuate_words("x1_%d" % c, x1t_g[c][:], eng)
@@ -99,16 +103,19 @@ def tile_model_kernel(tc, x1, x2, out):
         def QX1(c):
             nc.vector.quantize_mx(out=x1t_c[c][:].bitcast(FP8X4), scales=x1t_s[c][:], in_=x1t_g[c][:])
 
+        NR = 2
+        RW = D_LEN // NR
+
         def R(g, h, eng):
-            dst = x2k_g[g][:, 1024 * h:1024 * (h + 1)].rearrange("p (c i t) -> p c t i", i=4, t=4)
-            src = x2_sb[g][:].rearrange("p (t d) -> p t d", t=4)[:, :, 256 * h:256 * (h + 1)]
+            dst = x2k_g[g][:, 4 * RW * h:4 * RW * (h + 1)].rearrange("p (c i t) -> p c t i", i=4, t=4)
+            src = x2_sb[g][:].rearrange("p (t d) -> p t d", t=4)[:, :, RW * h:RW * (h + 1)]
             copy_on(eng, dst, src.rearrange("p t (c i) -> p c t i", i=4))
 
         def QK(g):
             nc.vector.quantize_mx(out=x2k_c[g][:].bitcast(FP8X4), scales=x2k_s[g][:], in_=x2k_g[g][:])
 
-        def A(i, h):
-            sp = psum.tile([P, 512], F32, name="s_%d_%d" % (i, h), tag="bank")
+        def A(i, h, bank):
+            sp = bank_tile("s_%d_%d" % (i, h), [P, 512], F32, bank)
             c, t = i // 2, i % 2
             nc.tensor.matmul_mx(
                 out=sp[:],
@@ -119,61 +126,73 @@ def tile_model_kernel(tc, x1, x2, out):
                 start=True,
                 stop=True,
             )
-            banks["s_%d_%d" % (i, h)] = sp
 
-        def B(i):
-            for h in range(2):
-                nc.vector.tensor_reduce(out=mx[i][:, h:h + 1], in_=banks["s_%d_%d" % (i, h)][:], axis=AX.X, op=ALU.max)
+        def B(i, h):
             nc.vector.tensor_scalar(
-                out=nb[i][:], in0=mx[i][:, 0:1], scalar1=mx[i][:, 1:2], scalar2=-SCALE, op0=ALU.max, op1=ALU.mult
+                out=sc[i][:, 512 * h:512 * (h + 1)],
+                in0=banks["s_%d_%d" % (i, h)][:],
+                scalar1=-SCALE,
+                scalar2=(None if h == 0 else t0[i][:]),
+                op0=ALU.mult,
+                op1=ALU.min,
+                accum_out=(t0[i][:] if h == 0 else nb[i][:]),
             )
 
         def C(i):
-            for h in range(2):
-                nc.scalar.activation(
-                    out=e_sb[i][:, 512 * h:512 * (h + 1)],
-                    in_=banks["s_%d_%d" % (i, h)][:],
-                    func=ACT.Exp,
-                    bias=nb[i][:],
-                    scale=SCALE,
-                    accum_out=rs[i][:, h:h + 1],
-                )
+            nc.scalar.activation(
+                out=e_sb[i][:], in_=sc[i][:], func=ACT.Exp, bias=nb[i][:], scale=-1.0, accum_out=rs[i][:]
+            )
 
-        def Dh(i, g, et, col):
+        PLAIN = []
+
+        def flip(i, g, et, col):
             for j in range(4):
                 k0 = 512 * g + P * j
-                nc.tensor.transpose(et[:, col + P * j:col + P * (j + 1)], e_sb[i][:, k0:k0 + P], ident_b[:])
+                if i in PLAIN:
+                    nc.tensor.matmul(
+                        out=et[:, col:col + 512].rearrange("p (q j) -> p q j", j=4)[:, :, j],
+                        lhsT=e_sb[i][:, k0:k0 + P],
+                        rhs=ident_b[:],
+                        start=True,
+                        stop=True,
+                    )
+                else:
+                    nc.tensor.transpose(et[:, col + P * j:col + P * (j + 1)], e_sb[i][:, k0:k0 + P], ident_b[:])
 
-        def Dfull(i):
-            et = psum.tile([P, 1024], BF16, name="et_%d" % i, tag="bank")
-            Dh(i, 0, et, 0)
-            Dh(i, 1, et, 512)
-            banks["et_%d" % i] = et
+        def D(i, bank):
+            et = bank_tile("et_%d" % i, [P, 1024], BF16, bank)
+            flip(i, 0, et, 0)
+            flip(i, 1, et, 512)
 
-        def Efull(i, eng):
-            copy_on(
-                eng,
-                e_g[i][:].rearrange("p (g q j) -> p g q j", g=2, j=4),
-                banks["et_%d" % i][:].rearrange("p (g j q) -> p g q j", g=2, j=4),
-            )
+        def E(i, eng):
+            if i in PLAIN:
+                copy_on(eng, e_g[i][:], banks["et_%d" % i][:])
+            else:
+                copy_on(
+                    eng,
+                    e_g[i][:].rearrange("p (g q j) -> p g q j", g=2, j=4),
+                    banks["et_%d" % i][:].rearrange("p (g j q) -> p g q j", g=2, j=4),
+                )
 
-        def Dhalf(i, g):
-            et = psum.tile([P, 512], BF16, name="et_%d_%d" % (i, g), tag="bank")
-            Dh(i, g, et, 0)
-            banks["et_%d_%d" % (i, g)] = et
+        def Dh(i, g, bank):
+            et = bank_tile("et_%d_%d" % (i, g), [P, 512], BF16, bank)
+            flip(i, g, et, 0)
 
-        def Ehalf(i, g, eng):
-            copy_on(
-                eng,
-                e_g[i][:, 512 * g:512 * (g + 1)].rearrange("p (q j) -> p q j", j=4),
-                banks["et_%d_%d" % (i, g)][:].rearrange("p (j q) -> p q j", j=4),
-            )
+        def Eh(i, g, eng):
+            if i in PLAIN:
+                copy_on(eng, e_g[i][:, 512 * g:512 * (g + 1)], banks["et_%d_%d" % (i, g)][:])
+            else:
+                copy_on(
+                    eng,
+                    e_g[i][:, 512 * g:512 * (g + 1)].rearrange("p (q j) -> p q j", j=4),
+                    banks["et_%d_%d" % (i, g)][:].rearrange("p (j q) -> p q j", j=4),
+                )
 
         def F(i):
             nc.vector.quantize_mx(out=e_c[i][:].bitcast(FP8X4), scales=e_s[i][:], in_=e_g[i][:])
 
-        def G(i, c0, width):
-            op = psum.tile([P, width], F32, name="o_%d_%d" % (i, c0), tag="bank")
+        def G(i, c0, width, bank):
+            op = bank_tile("o_%d_%d" % (i, c0), [P, width], F32, bank)
             for g in range(2):
                 nc.tensor.matmul_mx(
                     out=op[:],
@@ -184,11 +203,9 @@ def tile_model_kernel(tc, x1, x2, out):
                     start=(g == 0),
                     stop=(g == 1),
                 )
-            banks["o_%d_%d" % (i, c0)] = op
 
         def Hs(i):
-            nc.vector.tensor_tensor(out=rt[i][:], in0=rs[i][:, 0:1], in1=rs[i][:, 1:2], op=ALU.add)
-            nc.vector.reciprocal(out=ri[i][:], in_=rt[i][:])
+            nc.vector.reciprocal(out=ri[i][:], in_=rs[i][:])
 
         def H(i, c0, width, eng):
             op = banks["o_%d_%d" % (i, c0)]
@@ -212,73 +229,123 @@ def tile_model_kernel(tc, x1, x2, out):
         for c in range(1, 4):
             nc.sync.dma_start(out=x1_sb[c][:], in_=x1v[:, 1024 * c:1024 * (c + 1)])
 
-        PX2(0, 0)
-        PX2(0, 1)
-        EX2(0, 0, "V")
+        PX2(0, 0, 0)
+        PX2(0, 1, 1)
+        PX1(0, 2)
+        PX2(1, 0, 3)
+        PX2(1, 1, 4)
+        PX1(1, 5)
+        PX1(2, 6)
+        PX1(3, 7)
+        R(0, 0, "V")
+        R(0, 1, "V")
+        QK(0)
+        EX2(0, 0, "S")
         EX2(0, 1, "S")
-        PX1(0)
         EX1(0, "S")
-        QX2(0)
-        QX1(0)
-        PX2(1, 0)
-        PX2(1, 1)
         EX2(1, 0, "S")
-        EX2(1, 1, "V")
-        PX1(1)
-        PX1(2)
-        A(0, 0)
-        A(1, 0)
-        QX2(1)
+        EX2(1, 1, "S")
         EX1(1, "S")
         EX1(2, "S")
-        A(0, 1)
-        A(1, 1)
-        PX1(3)
-        R(0, 0, "S")
-        B(0)
-        for n in range(NT + 2):
-            if n < NT:
-                C(n)
-            if 0 <= n - 1 < NT - 1:
-                Dfull(n - 1)
-            if n - 1 == NT - 1:
-                Dhalf(n - 1, 0)
-                Dhalf(n - 1, 1)
-            if 0 <= n - 2:
-                F(n - 2)
-            if n + 1 < NT:
-                B(n + 1)
-            if n == 0:
-                QX1(1)
-                R(0, 1, "V")
-                QK(0)
-                EX1(3, "S")
-            if n == 1:
-                R(1, 0, "V")
-                R(1, 1, "V")
-                QK(1)
-                QX1(2)
-            if n == 2:
-                QX1(3)
-            if n + 2 < NT:
-                A(n + 2, 0)
-                A(n + 2, 1)
-            if 0 <= n - 2 < NT - 1:
-                G(n - 2, 0, 512)
-            if n - 2 == NT - 1:
-                G(n - 2, 0, 256)
-                G(n - 2, 256, 256)
-            if 0 <= n - 1 < NT - 2:
-                Efull(n - 1, "S")
-            if n - 1 == NT - 2:
-                Efull(n - 1, "V")
-            if n - 1 == NT - 1:
-                Ehalf(n - 1, 0, "S")
-                Ehalf(n - 1, 1, "V")
-            if 0 <= n - 2:
-                Hs(n - 2)
-            if 0 <= n - 2 < NT - 1:
-                H(n - 2, 0, 512, "S" if n - 2 >= 5 else "V")
-            if n - 2 == NT - 1:
-                H(n - 2, 0, 256, "V")
-                H(n - 2, 256, 256, "S")
+        EX1(3, "S")
+        QX2(0)
+        QX1(0)
+        R(1, 0, "V")
+        QX2(1)
+        R(1, 1, "V")
+        QX1(1)
+        A(0, 0, 0)
+        A(0, 1, 1)
+        A(1, 0, 2)
+        A(1, 1, 3)
+        B(0, 0)
+        B(0, 1)
+        B(1, 0)
+        B(1, 1)
+        C(0)
+        C(1)
+        A(2, 0, 0)
+        A(2, 1, 1)
+        D(0, 4)
+        A(3, 0, 2)
+        A(3, 1, 3)
+        D(1, 5)
+        B(2, 0)
+        B(2, 1)
+        QX1(2)
+        QK(1)
+        B(3, 0)
+        B(3, 1)
+        QX1(3)
+        C(2)
+        E(0, "S")
+        C(3)
+        E(1, "S")
+        A(4, 0, 0)
+        A(4, 1, 1)
+        D(2, 4)
+        A(5, 0, 2)
+        A(5, 1, 3)
+        B(4, 0)
+        B(4, 1)
+        F(0)
+        Hs(0)
+        B(5, 0)
+        B(5, 1)
+        F(1)
+        Hs(1)
+        C(4)
+        E(2, "S")
+        G(0, 0, 512, 6)
+        D(3, 5)
+        A(6, 0, 0)
+        A(6, 1, 1)
+        G(1, 0, 512, 7)
+        D(4, 4)
+        A(7, 0, 2)
+        A(7, 1, 3)
+        B(6, 0)
+        B(6, 1)
+        F(2)
+        Hs(2)
+        B(7, 0)
+        B(7, 1)
+        H(0, 0, 512, "S")
+        C(5)
+        E(3, "S")
+        H(1, 0, 512, "S")
+        C(6)
+        G(2, 0, 512, 6)
+        D(5, 5)
+        F(3)
+        Hs(3)
+        E(4, "V")
+        F(4)
+        Hs(4)
+        E(5, "V")
+        F(5)
+        Hs(5)
+        H(2, 0, 512, "S")
+        C(7)
+        G(3, 0, 512, 7)
+        D(6, 4)
+        G(4, 0, 512, 6)
+        Dh(7, 0, 5)
+        Dh(7, 1, 0)
+        E(6, "V")
+        F(6)
+        Hs(6)
+        Eh(7, 1, "V")
+        H(3, 0, 512, "S")
+        H(4, 0, 512, "S")
+        Eh(7, 0, "S")
+        G(5, 0, 512, 7)
+        G(6, 0, 512, 6)
+        F(7)
+        Hs(7)
+        H(5, 0, 512, "S")
+        H(6, 0, 512, "S")
+        G(7, 0, 256, 7)
+        G(7, 256, 256, 1)
+        H(7, 0, 256, "V")
+        H(7, 256, 256, "S")

@@ -246,13 +246,13 @@ def tile_model_kernel(tc, x1, x2, out):
         EX2(1, 0, "S")
         EX2(1, 1, "S")
         EX1(1, "S")
+        R(1, 1, "S")
         EX1(2, "S")
         EX1(3, "S")
         QX2(0)
         QX1(0)
         R(1, 0, "V")
         QX2(1)
-        R(1, 1, "V")
         QX1(1)
         A(0, 0, 0)
         A(0, 1, 1)
@@ -266,10 +266,9 @@ def tile_model_kernel(tc, x1, x2, out):
         C(1)
         A(2, 0, 0)
         A(2, 1, 1)
-        D(0, 4)
         A(3, 0, 2)
         A(3, 1, 3)
-        D(1, 5)
+        D(0, 4)
         B(2, 0)
         B(2, 1)
         QX1(2)
@@ -280,65 +279,66 @@ def tile_model_kernel(tc, x1, x2, out):
         C(2)
         E(0, "S")
         C(3)
-        E(1, "S")
         A(4, 0, 0)
         A(4, 1, 1)
-        D(2, 4)
+        D(1, 5)
         A(5, 0, 2)
         A(5, 1, 3)
+        D(2, 4)
         B(4, 0)
         B(4, 1)
-        F(0)
-        Hs(0)
         B(5, 0)
         B(5, 1)
-        F(1)
-        Hs(1)
+        F(0)
+        Hs(0)
+        E(1, "S")
         C(4)
         E(2, "S")
-        G(0, 0, 512, 6)
-        D(3, 5)
+        C(5)
         A(6, 0, 0)
         A(6, 1, 1)
-        G(1, 0, 512, 7)
-        D(4, 4)
+        D(3, 5)
+        G(0, 0, 512, 6)
         A(7, 0, 2)
         A(7, 1, 3)
+        D(4, 4)
         B(6, 0)
         B(6, 1)
-        F(2)
-        Hs(2)
+        F(1)
+        Hs(1)
         B(7, 0)
         B(7, 1)
-        H(0, 0, 512, "S")
-        C(5)
-        E(3, "S")
-        H(1, 0, 512, "S")
-        C(6)
-        G(2, 0, 512, 6)
-        D(5, 5)
+        E(3, "V")
+        F(2)
+        Hs(2)
+        E(4, "V")
         F(3)
         Hs(3)
-        E(4, "V")
+        H(0, 0, 512, "S")
+        C(6)
+        G(1, 0, 512, 7)
+        D(5, 5)
+        G(2, 0, 512, 6)
+        D(6, 4)
+        E(5, "V")
         F(4)
         Hs(4)
-        E(5, "V")
         F(5)
         Hs(5)
-        H(2, 0, 512, "S")
+        H(1, 0, 512, "S")
         C(7)
+        H(2, 0, 512, "S")
+        E(6, "S")
         G(3, 0, 512, 7)
-        D(6, 4)
-        G(4, 0, 512, 6)
         Dh(7, 0, 5)
         Dh(7, 1, 0)
-        E(6, "V")
+        G(4, 0, 512, 6)
+        H(3, 0, 512, "V")
+        Eh(7, 1, "V")
         F(6)
         Hs(6)
-        Eh(7, 1, "V")
-        H(3, 0, 512, "S")
-        H(4, 0, 512, "S")
         Eh(7, 0, "S")
+        H(4, 0, 512, "S")
         G(5, 0, 512, 7)
         G(6, 0, 512, 6)
         F(7)

@@ -25,7 +25,6 @@ def tile_model_kernel(tc, x1, x2, out):
     with ExitStack() as ctx:
         keep = ctx.enter_context(tc.tile_pool(name="keep", bufs=1))
         psum = ctx.enter_context(tc.psum_pool(name="psum", bufs=1))
-        ctx.enter_context(tc.manual_schedule())
 
         x2v = x2.flatten_outer_dims().rearrange("(g p j) d -> p g (j d)", g=2, p=P, j=4)
         x1v = x1.flatten_outer_dims().rearrange("(p i) d -> p (i d)", i=NT)

@@ -16,8 +16,17 @@ P = 128
 S_LEN = 1024
 D_LEN = 512
 NT = S_LEN // P
+LAST = NT - 1
 SCALE = 1.0 / math.sqrt(D_LEN)
 FLOPS = 2 * 2 * S_LEN * S_LEN * D_LEN
+
+EXP_AHEAD = 2
+SCORES_AHEAD = 3
+QUANT_BEHIND = 1
+OUT_BEHIND = 2
+
+E_COPY_ON_VECTOR = (3, 4, 5)
+OUT_ON_VECTOR = (3,)
 
 
 def tile_model_kernel(tc, x1, x2, out):
@@ -32,8 +41,8 @@ def tile_model_kernel(tc, x1, x2, out):
 
         ident_f = keep.tile([P, P], F32, name="ident_f")
         ident_b = keep.tile([P, P], BF16, name="ident_b")
-        warm = keep.tile([P, 1], F32, name="warm")
-        warm2 = keep.tile([P, 1], F32, name="warm2")
+        zero = keep.tile([P, 1], F32, name="zero")
+        one = keep.tile([P, 1], F32, name="one")
 
         x2_sb = [keep.tile([P, 4 * D_LEN], BF16, name="x2_sb%d" % g) for g in range(2)]
         x1_sb = [keep.tile([P, 2 * D_LEN], BF16, name="x1_sb%d" % c) for c in range(4)]
@@ -46,151 +55,123 @@ def tile_model_kernel(tc, x1, x2, out):
         x2k_g = [keep.tile([P, 2048], BF16, name="x2k_g%d" % g, align_bytes=64) for g in range(2)]
         x2k_c = [keep.tile([P, 512], U32, name="x2k_c%d" % g, align_bytes=64) for g in range(2)]
         x2k_s = [keep.tile([P, 512], U8, name="x2k_s%d" % g, align_bytes=64) for g in range(2)]
-        sc = [keep.tile([P, S_LEN], F32, name="sc%d" % i) for i in range(NT)]
+        neg_s = [keep.tile([P, S_LEN], F32, name="neg_s%d" % i) for i in range(NT)]
         e_sb = [keep.tile([P, S_LEN], BF16, name="e_sb%d" % i) for i in range(NT)]
         e_g = [keep.tile([P, S_LEN], BF16, name="e_g%d" % i, align_bytes=64) for i in range(NT)]
         e_c = [keep.tile([P, 256], U32, name="e_c%d" % i, align_bytes=64) for i in range(NT)]
         e_s = [keep.tile([P, 256], U8, name="e_s%d" % i, align_bytes=64) for i in range(NT)]
         o_sb = [keep.tile([P, D_LEN], F32, name="o_sb%d" % i) for i in range(NT)]
-        t0 = [keep.tile([P, 1], F32, name="t0_%d" % i) for i in range(NT)]
-        nb = [keep.tile([P, 1], F32, name="nb%d" % i) for i in range(NT)]
-        rs = [keep.tile([P, 1], F32, name="rs%d" % i) for i in range(NT)]
-        ri = [keep.tile([P, 1], F32, name="ri%d" % i) for i in range(NT)]
+        half_min = [keep.tile([P, 1], F32, name="half_min%d" % i) for i in range(NT)]
+        neg_max = [keep.tile([P, 1], F32, name="neg_max%d" % i) for i in range(NT)]
+        row_sum = [keep.tile([P, 1], F32, name="row_sum%d" % i) for i in range(NT)]
+        inv_sum = [keep.tile([P, 1], F32, name="inv_sum%d" % i) for i in range(NT)]
 
-        banks = {}
+        in_bank = {}
 
         def bank_tile(key, shape, dtype, bank):
-            t = psum.tile(shape, dtype, name="ps_" + key, tag="bank%d" % bank)
-            banks[key] = t
-            return t
+            in_bank[key] = psum.tile(shape, dtype, name="ps_" + key, tag="bank%d" % bank)
+            return in_bank[key]
 
-        def copy_on(eng, dst, src):
-            if eng == "V":
+        def copy_on(vector, dst, src):
+            if vector:
                 nc.vector.tensor_copy(out=dst, in_=src)
-            elif eng == "S":
-                nc.scalar.copy(out=dst, in_=src)
             else:
-                nc.gpsimd.tensor_scalar(out=dst, in0=src, scalar1=1.0, scalar2=0.0, op0=ALU.mult, op1=ALU.add)
+                nc.scalar.copy(out=dst, in_=src)
 
-        def transpose_words(key, src_words, bank):
+        def transpose_rows(key, rows, bank):
+            words = rows.bitcast(F32)
             xt = bank_tile(key, [P, 512], F32, bank)
             for s in range(4):
-                nc.tensor.transpose(xt[:, P * s:P * (s + 1)], src_words[:, P * s:P * (s + 1)], ident_f[:])
+                nc.tensor.transpose(xt[:, P * s:P * (s + 1)], words[:, P * s:P * (s + 1)], ident_f[:])
 
-        def evacuate_words(key, dst_bf16, eng):
+        def group_features(key, dst, vector):
             copy_on(
-                eng,
-                dst_bf16.bitcast(F32).rearrange("p (t r u) -> p t r u", t=2, u=2),
-                banks[key][:].rearrange("p (t u r) -> p t r u", t=2, u=2),
+                vector,
+                dst.bitcast(F32).rearrange("p (t r u) -> p t r u", t=2, u=2),
+                in_bank[key][:].rearrange("p (t u r) -> p t r u", t=2, u=2),
             )
 
-        def PX2(g, b, bank):
-            transpose_words("x2_%d_%d" % (g, b), x2_sb[g][:].bitcast(F32)[:, 512 * b:512 * (b + 1)], bank)
+        def quantise(codes, scales, values):
+            nc.vector.quantize_mx(out=codes.bitcast(FP8X4), scales=scales, in_=values)
 
-        def EX2(g, b, eng):
-            evacuate_words("x2_%d_%d" % (g, b), x2t_g[g][:, 1024 * b:1024 * (b + 1)], eng)
+        def x2_transpose(g, b, bank):
+            transpose_rows("x2_%d_%d" % (g, b), x2_sb[g][:, 1024 * b:1024 * (b + 1)], bank)
 
-        def QX2(g):
-            nc.vector.quantize_mx(out=x2t_c[g][:].bitcast(FP8X4), scales=x2t_s[g][:], in_=x2t_g[g][:])
+        def x2_group(g, b):
+            group_features("x2_%d_%d" % (g, b), x2t_g[g][:, 1024 * b:1024 * (b + 1)], False)
 
-        def PX1(c, bank):
-            transpose_words("x1_%d" % c, x1_sb[c][:].bitcast(F32), bank)
+        def x1_transpose(c, bank):
+            transpose_rows("x1_%d" % c, x1_sb[c][:], bank)
 
-        def EX1(c, eng):
-            evacuate_words("x1_%d" % c, x1t_g[c][:], eng)
+        def x1_group(c):
+            group_features("x1_%d" % c, x1t_g[c][:], False)
 
-        def QX1(c):
-            nc.vector.quantize_mx(out=x1t_c[c][:].bitcast(FP8X4), scales=x1t_s[c][:], in_=x1t_g[c][:])
+        def x2_group_keys(g, h, vector):
+            dst = x2k_g[g][:, 1024 * h:1024 * (h + 1)].rearrange("p (c i j) -> p c j i", i=4, j=4)
+            src = x2_sb[g][:].rearrange("p (j d) -> p j d", j=4)[:, :, 256 * h:256 * (h + 1)]
+            copy_on(vector, dst, src.rearrange("p j (c i) -> p c j i", i=4))
 
-        NR = 2
-        RW = D_LEN // NR
-
-        def R(g, h, eng):
-            dst = x2k_g[g][:, 4 * RW * h:4 * RW * (h + 1)].rearrange("p (c i t) -> p c t i", i=4, t=4)
-            src = x2_sb[g][:].rearrange("p (t d) -> p t d", t=4)[:, :, RW * h:RW * (h + 1)]
-            copy_on(eng, dst, src.rearrange("p t (c i) -> p c t i", i=4))
-
-        def QK(g):
-            nc.vector.quantize_mx(out=x2k_c[g][:].bitcast(FP8X4), scales=x2k_s[g][:], in_=x2k_g[g][:])
-
-        def A(i, h, bank):
-            sp = bank_tile("s_%d_%d" % (i, h), [P, 512], F32, bank)
+        def scores(i):
             c, t = i // 2, i % 2
-            nc.tensor.matmul_mx(
-                out=sp[:],
-                lhsT=x1t_c[c][:, P * t:P * (t + 1)].bitcast(FP8X4),
-                lhsT_scale=x1t_s[c][:, P * t:P * (t + 1)],
-                rhs=x2t_c[h][:].bitcast(FP8X4),
-                rhs_scale=x2t_s[h][:],
-                start=True,
-                stop=True,
-            )
+            for h in range(2):
+                sp = bank_tile("s_%d_%d" % (i, h), [P, 512], F32, (2 * i + h) % 4)
+                nc.tensor.matmul_mx(
+                    out=sp[:],
+                    lhsT=x1t_c[c][:, P * t:P * (t + 1)].bitcast(FP8X4),
+                    lhsT_scale=x1t_s[c][:, P * t:P * (t + 1)],
+                    rhs=x2t_c[h][:].bitcast(FP8X4),
+                    rhs_scale=x2t_s[h][:],
+                    start=True,
+                    stop=True,
+                )
 
-        def B(i, h):
-            nc.vector.tensor_scalar(
-                out=sc[i][:, 512 * h:512 * (h + 1)],
-                in0=banks["s_%d_%d" % (i, h)][:],
-                scalar1=-SCALE,
-                scalar2=(None if h == 0 else t0[i][:]),
-                op0=ALU.mult,
-                op1=ALU.min,
-                accum_out=(t0[i][:] if h == 0 else nb[i][:]),
-            )
+        def scale_and_maximum(i):
+            for h in range(2):
+                nc.vector.tensor_scalar(
+                    out=neg_s[i][:, 512 * h:512 * (h + 1)],
+                    in0=in_bank["s_%d_%d" % (i, h)][:],
+                    scalar1=-SCALE,
+                    scalar2=(None if h == 0 else half_min[i][:]),
+                    op0=ALU.mult,
+                    op1=ALU.min,
+                    accum_out=(half_min[i][:] if h == 0 else neg_max[i][:]),
+                )
 
-        def C(i):
+        def exponential(i):
             nc.scalar.activation(
-                out=e_sb[i][:], in_=sc[i][:], func=ACT.Exp, bias=nb[i][:], scale=-1.0, accum_out=rs[i][:]
+                out=e_sb[i][:], in_=neg_s[i][:], func=ACT.Exp, bias=neg_max[i][:], scale=-1.0, accum_out=row_sum[i][:]
             )
 
-        PLAIN = []
-
-        def flip(i, g, et, col):
+        def transpose_e(i, g, et, col):
             for j in range(4):
                 k0 = 512 * g + P * j
-                if i in PLAIN:
-                    nc.tensor.matmul(
-                        out=et[:, col:col + 512].rearrange("p (q j) -> p q j", j=4)[:, :, j],
-                        lhsT=e_sb[i][:, k0:k0 + P],
-                        rhs=ident_b[:],
-                        start=True,
-                        stop=True,
-                    )
-                else:
-                    nc.tensor.transpose(et[:, col + P * j:col + P * (j + 1)], e_sb[i][:, k0:k0 + P], ident_b[:])
+                nc.tensor.transpose(et[:, col + P * j:col + P * (j + 1)], e_sb[i][:, k0:k0 + P], ident_b[:])
 
-        def D(i, bank):
-            et = bank_tile("et_%d" % i, [P, 1024], BF16, bank)
-            flip(i, 0, et, 0)
-            flip(i, 1, et, 512)
-
-        def E(i, eng):
-            if i in PLAIN:
-                copy_on(eng, e_g[i][:], banks["et_%d" % i][:])
+        def keys_to_partitions(i):
+            if i < LAST:
+                et = bank_tile("et_%d" % i, [P, 1024], BF16, 4 + i % 2)
+                transpose_e(i, 0, et, 0)
+                transpose_e(i, 1, et, 512)
             else:
+                transpose_e(i, 0, bank_tile("et_%d_0" % i, [P, 512], BF16, 4 + i % 2), 0)
+                transpose_e(i, 1, bank_tile("et_%d_1" % i, [P, 512], BF16, 0), 0)
+
+        def group_keys(i):
+            if i < LAST:
                 copy_on(
-                    eng,
+                    i in E_COPY_ON_VECTOR,
                     e_g[i][:].rearrange("p (g q j) -> p g q j", g=2, j=4),
-                    banks["et_%d" % i][:].rearrange("p (g j q) -> p g q j", g=2, j=4),
+                    in_bank["et_%d" % i][:].rearrange("p (g j q) -> p g q j", g=2, j=4),
                 )
-
-        def Dh(i, g, bank):
-            et = bank_tile("et_%d_%d" % (i, g), [P, 512], BF16, bank)
-            flip(i, g, et, 0)
-
-        def Eh(i, g, eng):
-            if i in PLAIN:
-                copy_on(eng, e_g[i][:, 512 * g:512 * (g + 1)], banks["et_%d_%d" % (i, g)][:])
             else:
-                copy_on(
-                    eng,
-                    e_g[i][:, 512 * g:512 * (g + 1)].rearrange("p (q j) -> p q j", j=4),
-                    banks["et_%d_%d" % (i, g)][:].rearrange("p (j q) -> p q j", j=4),
-                )
+                for g in range(2):
+                    copy_on(
+                        g == 1,
+                        e_g[i][:, 512 * g:512 * (g + 1)].rearrange("p (q j) -> p q j", j=4),
+                        in_bank["et_%d_%d" % (i, g)][:].rearrange("p (j q) -> p q j", j=4),
+                    )
 
-        def F(i):
-            nc.vector.quantize_mx(out=e_c[i][:].bitcast(FP8X4), scales=e_s[i][:], in_=e_g[i][:])
-
-        def G(i, c0, width, bank):
+        def weighted_sum(i, c0, width, bank):
             op = bank_tile("o_%d_%d" % (i, c0), [P, width], F32, bank)
             for g in range(2):
                 nc.tensor.matmul_mx(
@@ -203,20 +184,33 @@ def tile_model_kernel(tc, x1, x2, out):
                     stop=(g == 1),
                 )
 
-        def Hs(i):
-            nc.vector.reciprocal(out=ri[i][:], in_=rs[i][:])
-
-        def H(i, c0, width, eng):
-            op = banks["o_%d_%d" % (i, c0)]
-            dst = o_sb[i][:, c0:c0 + width]
-            if eng == "V":
-                nc.vector.tensor_scalar(out=dst, in0=op[:], scalar1=ri[i][:], scalar2=None, op0=ALU.mult)
+        def second_matmul(i):
+            quantise(e_c[i][:], e_s[i][:], e_g[i][:])
+            nc.vector.reciprocal(out=inv_sum[i][:], in_=row_sum[i][:])
+            if i < LAST:
+                weighted_sum(i, 0, 512, 6 + i % 2)
             else:
-                nc.scalar.activation(out=dst, in_=op[:], func=ACT.Copy, scale=ri[i][:])
+                weighted_sum(i, 0, 256, 6 + i % 2)
+                weighted_sum(i, 256, 256, 1)
+
+        def divide_and_store(i, c0, width, vector):
+            op = in_bank["o_%d_%d" % (i, c0)]
+            dst = o_sb[i][:, c0:c0 + width]
+            if vector:
+                nc.vector.tensor_scalar(out=dst, in0=op[:], scalar1=inv_sum[i][:], scalar2=None, op0=ALU.mult)
+            else:
+                nc.scalar.activation(out=dst, in_=op[:], func=ACT.Copy, scale=inv_sum[i][:])
             nc.sync.dma_start(out=outv[:, i, c0:c0 + width], in_=dst)
 
-        nc.vector.memset(warm[:], 0.0)
-        nc.scalar.activation(out=warm2[:], in_=warm[:], func=ACT.Exp)
+        def output(i):
+            if i < LAST:
+                divide_and_store(i, 0, 512, i in OUT_ON_VECTOR)
+            else:
+                divide_and_store(i, 0, 256, True)
+                divide_and_store(i, 256, 256, False)
+
+        nc.vector.memset(zero[:], 0.0)
+        nc.scalar.activation(out=one[:], in_=zero[:], func=ACT.Exp)
         make_identity(nc, ident_f[:])
         make_identity(nc, ident_b[:])
 
@@ -228,123 +222,52 @@ def tile_model_kernel(tc, x1, x2, out):
         for c in range(1, 4):
             nc.sync.dma_start(out=x1_sb[c][:], in_=x1v[:, 1024 * c:1024 * (c + 1)])
 
-        PX2(0, 0, 0)
-        PX2(0, 1, 1)
-        PX1(0, 2)
-        PX2(1, 0, 3)
-        PX2(1, 1, 4)
-        PX1(1, 5)
-        PX1(2, 6)
-        PX1(3, 7)
-        R(0, 0, "V")
-        R(0, 1, "V")
-        QK(0)
-        EX2(0, 0, "S")
-        EX2(0, 1, "S")
-        EX1(0, "S")
-        EX2(1, 0, "S")
-        EX2(1, 1, "S")
-        EX1(1, "S")
-        R(1, 1, "S")
-        EX1(2, "S")
-        EX1(3, "S")
-        QX2(0)
-        QX1(0)
-        R(1, 0, "V")
-        QX2(1)
-        QX1(1)
-        A(0, 0, 0)
-        A(0, 1, 1)
-        A(1, 0, 2)
-        A(1, 1, 3)
-        B(0, 0)
-        B(0, 1)
-        B(1, 0)
-        B(1, 1)
-        C(0)
-        C(1)
-        A(2, 0, 0)
-        A(2, 1, 1)
-        A(3, 0, 2)
-        A(3, 1, 3)
-        D(0, 4)
-        B(2, 0)
-        B(2, 1)
-        QX1(2)
-        QK(1)
-        B(3, 0)
-        B(3, 1)
-        QX1(3)
-        C(2)
-        E(0, "S")
-        C(3)
-        A(4, 0, 0)
-        A(4, 1, 1)
-        D(1, 5)
-        A(5, 0, 2)
-        A(5, 1, 3)
-        D(2, 4)
-        B(4, 0)
-        B(4, 1)
-        B(5, 0)
-        B(5, 1)
-        F(0)
-        Hs(0)
-        E(1, "S")
-        C(4)
-        E(2, "S")
-        C(5)
-        A(6, 0, 0)
-        A(6, 1, 1)
-        D(3, 5)
-        G(0, 0, 512, 6)
-        A(7, 0, 2)
-        A(7, 1, 3)
-        D(4, 4)
-        B(6, 0)
-        B(6, 1)
-        F(1)
-        Hs(1)
-        B(7, 0)
-        B(7, 1)
-        E(3, "V")
-        F(2)
-        Hs(2)
-        E(4, "V")
-        F(3)
-        Hs(3)
-        H(0, 0, 512, "S")
-        C(6)
-        G(1, 0, 512, 7)
-        D(5, 5)
-        G(2, 0, 512, 6)
-        D(6, 4)
-        E(5, "V")
-        F(4)
-        Hs(4)
-        F(5)
-        Hs(5)
-        H(1, 0, 512, "S")
-        C(7)
-        H(2, 0, 512, "S")
-        E(6, "S")
-        G(3, 0, 512, 7)
-        Dh(7, 0, 5)
-        Dh(7, 1, 0)
-        G(4, 0, 512, 6)
-        H(3, 0, 512, "V")
-        Eh(7, 1, "V")
-        F(6)
-        Hs(6)
-        Eh(7, 0, "S")
-        H(4, 0, 512, "S")
-        G(5, 0, 512, 7)
-        G(6, 0, 512, 6)
-        F(7)
-        Hs(7)
-        H(5, 0, 512, "S")
-        H(6, 0, 512, "S")
-        G(7, 0, 256, 7)
-        G(7, 256, 256, 1)
-        H(7, 0, 256, "V")
-        H(7, 256, 256, "S")
+        x2_transpose(0, 0, 0)
+        x2_transpose(0, 1, 1)
+        x1_transpose(0, 2)
+        x2_transpose(1, 0, 3)
+        x2_transpose(1, 1, 4)
+        for c in range(1, 4):
+            x1_transpose(c, 4 + c)
+
+        x2_group_keys(0, 0, True)
+        x2_group_keys(0, 1, True)
+        quantise(x2k_c[0][:], x2k_s[0][:], x2k_g[0][:])
+        x2_group(0, 0)
+        x2_group(0, 1)
+        x1_group(0)
+        x2_group(1, 0)
+        x2_group(1, 1)
+        x1_group(1)
+        x1_group(2)
+        x1_group(3)
+        quantise(x2t_c[0][:], x2t_s[0][:], x2t_g[0][:])
+        quantise(x1t_c[0][:], x1t_s[0][:], x1t_g[0][:])
+        x2_group_keys(1, 0, True)
+        quantise(x2t_c[1][:], x2t_s[1][:], x2t_g[1][:])
+        x2_group_keys(1, 1, True)
+        quantise(x1t_c[1][:], x1t_s[1][:], x1t_g[1][:])
+
+        for i in range(SCORES_AHEAD):
+            scores(i)
+            scale_and_maximum(i)
+        quantise(x1t_c[2][:], x1t_s[2][:], x1t_g[2][:])
+        quantise(x2k_c[1][:], x2k_s[1][:], x2k_g[1][:])
+        quantise(x1t_c[3][:], x1t_s[3][:], x1t_g[3][:])
+
+        def in_range(i):
+            return 0 <= i < NT
+
+        for n in range(-EXP_AHEAD, NT + QUANT_BEHIND + OUT_BEHIND):
+            if in_range(n - QUANT_BEHIND - OUT_BEHIND):
+                output(n - QUANT_BEHIND - OUT_BEHIND)
+            if in_range(n):
+                group_keys(n)
+            if in_range(n - QUANT_BEHIND):
+                second_matmul(n - QUANT_BEHIND)
+            if SCORES_AHEAD <= n + EXP_AHEAD + SCORES_AHEAD < NT:
+                scores(n + EXP_AHEAD + SCORES_AHEAD)
+                scale_and_maximum(n + EXP_AHEAD + SCORES_AHEAD)
+            if in_range(n + EXP_AHEAD):
+                exponential(n + EXP_AHEAD)
+                keys_to_partitions(n + EXP_AHEAD)

@@ -142,34 +142,34 @@ def tile_model_kernel(tc, x1, x2, out):
                 out=e_sb[i][:], in_=neg_s[i][:], func=ACT.Exp, bias=neg_max[i][:], scale=-1.0, accum_out=row_sum[i][:]
             )
 
-        def transpose_e(i, g, et, col):
+        def transpose_e(i, g, et, first, step):
             for j in range(4):
                 k0 = 512 * g + P * j
-                nc.tensor.transpose(et[:, col + P * j:col + P * (j + 1)], e_sb[i][:, k0:k0 + P], ident_b[:])
+                col = first + step * j
+                nc.tensor.transpose(et[:, col:col + P], e_sb[i][:, k0:k0 + P], ident_b[:])
 
         def keys_to_partitions(i):
             if i < LAST:
                 et = bank_tile("et_%d" % i, [P, 1024], BF16, 4 + i % 2)
-                transpose_e(i, 0, et, 0)
-                transpose_e(i, 1, et, 512)
+                transpose_e(i, 0, et, 0, 2 * P)
+                transpose_e(i, 1, et, P, 2 * P)
             else:
-                transpose_e(i, 0, bank_tile("et_%d_0" % i, [P, 512], BF16, 4 + i % 2), 0)
-                transpose_e(i, 1, bank_tile("et_%d_1" % i, [P, 512], BF16, 0), 0)
+                transpose_e(i, 0, bank_tile("et_%d_0" % i, [P, 512], BF16, 4 + i % 2), 0, P)
+                transpose_e(i, 1, bank_tile("et_%d_1" % i, [P, 512], BF16, 0), 0, P)
+
+        def interleave(vector, dst, planes):
+            copy_on(
+                vector,
+                dst.rearrange("p (c i j) -> p c j i", i=4, j=4),
+                planes.rearrange("p (j c i) -> p c j i", j=4, i=4),
+            )
 
         def group_keys(i):
             if i < LAST:
-                copy_on(
-                    i in E_COPY_ON_VECTOR,
-                    e_g[i][:].rearrange("p (g q j) -> p g q j", g=2, j=4),
-                    in_bank["et_%d" % i][:].rearrange("p (g j q) -> p g q j", g=2, j=4),
-                )
+                interleave(i in E_COPY_ON_VECTOR, e_g[i][:], in_bank["et_%d" % i][:])
             else:
                 for g in range(2):
-                    copy_on(
-                        g == 1,
-                        e_g[i][:, 512 * g:512 * (g + 1)].rearrange("p (q j) -> p q j", j=4),
-                        in_bank["et_%d_%d" % (i, g)][:].rearrange("p (j q) -> p q j", j=4),
-                    )
+                    interleave(g == 1, e_g[i][:, 512 * g:512 * (g + 1)], in_bank["et_%d_%d" % (i, g)][:])
 
         def weighted_sum(i, c0, width, bank):
             op = bank_tile("o_%d_%d" % (i, c0), [P, width], F32, bank)

import math
from contextlib import ExitStack

import concourse.mybir as mybir
from concourse.masks import make_identity

F32 = mybir.dt.float32
BF16 = mybir.dt.bfloat16
U32 = mybir.dt.uint32
U8 = mybir.dt.uint8
FP8X4 = mybir.dt.float8_e4m3fn_x4
ACT = mybir.ActivationFunctionType
ALU = mybir.AluOpType

P = 128
S_LEN = 1024
D_LEN = 512
NT = S_LEN // P
LAST = NT - 1
SCALE = 1.0 / math.sqrt(D_LEN)
FLOPS = 2 * 2 * S_LEN * S_LEN * D_LEN

EXP_AHEAD = 2
SCORES_AHEAD = 3
QUANT_BEHIND = 1
OUT_BEHIND = 2

E_COPY_ON_VECTOR = (3, 4, 5)
OUT_ON_VECTOR = (3,)


def tile_model_kernel(tc, x1, x2, out):
    nc = tc.nc
    with ExitStack() as ctx:
        keep = ctx.enter_context(tc.tile_pool(name="keep", bufs=1))
        psum = ctx.enter_context(tc.psum_pool(name="psum", bufs=1))

        x2v = x2.flatten_outer_dims().rearrange("(g p j) d -> p g (j d)", g=2, p=P, j=4)
        x1v = x1.flatten_outer_dims().rearrange("(p i) d -> p (i d)", i=NT)
        outv = out.flatten_outer_dims().rearrange("(p i) d -> p i d", i=NT)

        ident_f = keep.tile([P, P], F32, name="ident_f")
        ident_b = keep.tile([P, P], BF16, name="ident_b")
        zero = keep.tile([P, 1], F32, name="zero")
        one = keep.tile([P, 1], F32, name="one")

        x2_sb = [keep.tile([P, 4 * D_LEN], BF16, name="x2_sb%d" % g) for g in range(2)]
        x1_sb = [keep.tile([P, 2 * D_LEN], BF16, name="x1_sb%d" % c) for c in range(4)]
        x2t_g = [keep.tile([P, 2048], BF16, name="x2t_g%d" % g, align_bytes=64) for g in range(2)]
        x2t_c = [keep.tile([P, 512], U32, name="x2t_c%d" % g, align_bytes=64) for g in range(2)]
        x2t_s = [keep.tile([P, 512], U8, name="x2t_s%d" % g, align_bytes=64) for g in range(2)]
        x1t_g = [keep.tile([P, 1024], BF16, name="x1t_g%d" % c, align_bytes=64) for c in range(4)]
        x1t_c = [keep.tile([P, 256], U32, name="x1t_c%d" % c, align_bytes=64) for c in range(4)]
        x1t_s = [keep.tile([P, 256], U8, name="x1t_s%d" % c, align_bytes=64) for c in range(4)]
        x2k_g = [keep.tile([P, 2048], BF16, name="x2k_g%d" % g, align_bytes=64) for g in range(2)]
        x2k_c = [keep.tile([P, 512], U32, name="x2k_c%d" % g, align_bytes=64) for g in range(2)]
        x2k_s = [keep.tile([P, 512], U8, name="x2k_s%d" % g, align_bytes=64) for g in range(2)]
        neg_s = [keep.tile([P, S_LEN], F32, name="neg_s%d" % i) for i in range(NT)]
        e_sb = [keep.tile([P, S_LEN], BF16, name="e_sb%d" % i) for i in range(NT)]
        e_g = [keep.tile([P, S_LEN], BF16, name="e_g%d" % i, align_bytes=64) for i in range(NT)]
        e_c = [keep.tile([P, 256], U32, name="e_c%d" % i, align_bytes=64) for i in range(NT)]
        e_s = [keep.tile([P, 256], U8, name="e_s%d" % i, align_bytes=64) for i in range(NT)]
        o_sb = [keep.tile([P, D_LEN], F32, name="o_sb%d" % i) for i in range(NT)]
        half_min = [keep.tile([P, 1], F32, name="half_min%d" % i) for i in range(NT)]
        neg_max = [keep.tile([P, 1], F32, name="neg_max%d" % i) for i in range(NT)]
        row_sum = [keep.tile([P, 1], F32, name="row_sum%d" % i) for i in range(NT)]
        inv_sum = [keep.tile([P, 1], F32, name="inv_sum%d" % i) for i in range(NT)]

        in_bank = {}

        def bank_tile(key, shape, dtype, bank):
            in_bank[key] = psum.tile(shape, dtype, name="ps_" + key, tag="bank%d" % bank)
            return in_bank[key]

        def copy_on(vector, dst, src):
            if vector:
                nc.vector.tensor_copy(out=dst, in_=src)
            else:
                nc.scalar.copy(out=dst, in_=src)

        def transpose_rows(key, rows, bank):
            words = rows.bitcast(F32)
            xt = bank_tile(key, [P, 512], F32, bank)
            for s in range(4):
                nc.tensor.transpose(xt[:, P * s:P * (s + 1)], words[:, P * s:P * (s + 1)], ident_f[:])

        def group_features(key, dst, vector):
            copy_on(
                vector,
                dst.bitcast(F32).rearrange("p (t r u) -> p t r u", t=2, u=2),
                in_bank[key][:].rearrange("p (t u r) -> p t r u", t=2, u=2),
            )

        def quantise(codes, scales, values):
            nc.vector.quantize_mx(out=codes.bitcast(FP8X4), scales=scales, in_=values)

        def x2_transpose(g, b, bank):
            transpose_rows("x2_%d_%d" % (g, b), x2_sb[g][:, 1024 * b:1024 * (b + 1)], bank)

        def x2_group(g, b):
            group_features("x2_%d_%d" % (g, b), x2t_g[g][:, 1024 * b:1024 * (b + 1)], False)

        def x1_transpose(c, bank):
            transpose_rows("x1_%d" % c, x1_sb[c][:], bank)

        def x1_group(c):
            group_features("x1_%d" % c, x1t_g[c][:], False)

        def x2_group_keys(g, h, vector):
            dst = x2k_g[g][:, 1024 * h:1024 * (h + 1)].rearrange("p (c i j) -> p c j i", i=4, j=4)
            src = x2_sb[g][:].rearrange("p (j d) -> p j d", j=4)[:, :, 256 * h:256 * (h + 1)]
            copy_on(vector, dst, src.rearrange("p j (c i) -> p c j i", i=4))

        def scores(i):
            c, t = i // 2, i % 2
            for h in range(2):
                sp = bank_tile("s_%d_%d" % (i, h), [P, 512], F32, (2 * i + h) % 4)
                nc.tensor.matmul_mx(
                    out=sp[:],
                    lhsT=x1t_c[c][:, P * t:P * (t + 1)].bitcast(FP8X4),
                    lhsT_scale=x1t_s[c][:, P * t:P * (t + 1)],
                    rhs=x2t_c[h][:].bitcast(FP8X4),
                    rhs_scale=x2t_s[h][:],
                    start=True,
                    stop=True,
                )

        def scale_and_maximum(i):
            for h in range(2):
                nc.vector.tensor_scalar(
                    out=neg_s[i][:, 512 * h:512 * (h + 1)],
                    in0=in_bank["s_%d_%d" % (i, h)][:],
                    scalar1=-SCALE,
                    scalar2=(None if h == 0 else half_min[i][:]),
                    op0=ALU.mult,
                    op1=ALU.min,
                    accum_out=(half_min[i][:] if h == 0 else neg_max[i][:]),
                )

        def exponential(i):
            nc.scalar.activation(
                out=e_sb[i][:], in_=neg_s[i][:], func=ACT.Exp, bias=neg_max[i][:], scale=-1.0, accum_out=row_sum[i][:]
            )

        def transpose_e(i, g, et, first, step):
            for j in range(4):
                k0 = 512 * g + P * j
                col = first + step * j
                nc.tensor.transpose(et[:, col:col + P], e_sb[i][:, k0:k0 + P], ident_b[:])

        def keys_to_partitions(i):
            if i < LAST:
                et = bank_tile("et_%d" % i, [P, 1024], BF16, 4 + i % 2)
                transpose_e(i, 0, et, 0, 2 * P)
                transpose_e(i, 1, et, P, 2 * P)
            else:
                transpose_e(i, 0, bank_tile("et_%d_0" % i, [P, 512], BF16, 4 + i % 2), 0, P)
                transpose_e(i, 1, bank_tile("et_%d_1" % i, [P, 512], BF16, 0), 0, P)

        def interleave(vector, dst, planes):
            copy_on(
                vector,
                dst.rearrange("p (c i j) -> p c j i", i=4, j=4),
                planes.rearrange("p (j c i) -> p c j i", j=4, i=4),
            )

        def group_keys(i):
            if i < LAST:
                interleave(i in E_COPY_ON_VECTOR, e_g[i][:], in_bank["et_%d" % i][:])
            else:
                for g in range(2):
                    interleave(g == 1, e_g[i][:, 512 * g:512 * (g + 1)], in_bank["et_%d_%d" % (i, g)][:])

        def weighted_sum(i, c0, width, bank):
            op = bank_tile("o_%d_%d" % (i, c0), [P, width], F32, bank)
            for g in range(2):
                nc.tensor.matmul_mx(
                    out=op[:],
                    lhsT=e_c[i][:, P * g:P * (g + 1)].bitcast(FP8X4),
                    lhsT_scale=e_s[i][:, P * g:P * (g + 1)],
                    rhs=x2k_c[g][:, c0:c0 + width].bitcast(FP8X4),
                    rhs_scale=x2k_s[g][:, c0:c0 + width],
                    start=(g == 0),
                    stop=(g == 1),
                )

        def second_matmul(i):
            quantise(e_c[i][:], e_s[i][:], e_g[i][:])
            nc.vector.reciprocal(out=inv_sum[i][:], in_=row_sum[i][:])
            if i < LAST:
                weighted_sum(i, 0, 512, 6 + i % 2)
            else:
                weighted_sum(i, 0, 256, 6 + i % 2)
                weighted_sum(i, 256, 256, 1)

        def divide_and_store(i, c0, width, vector):
            op = in_bank["o_%d_%d" % (i, c0)]
            dst = o_sb[i][:, c0:c0 + width]
            if vector:
                nc.vector.tensor_scalar(out=dst, in0=op[:], scalar1=inv_sum[i][:], scalar2=None, op0=ALU.mult)
            else:
                nc.scalar.activation(out=dst, in_=op[:], func=ACT.Copy, scale=inv_sum[i][:])
            nc.sync.dma_start(out=outv[:, i, c0:c0 + width], in_=dst)

        def output(i):
            if i < LAST:
                divide_and_store(i, 0, 512, i in OUT_ON_VECTOR)
            else:
                divide_and_store(i, 0, 256, True)
                divide_and_store(i, 256, 256, False)

        nc.vector.memset(zero[:], 0.0)
        nc.scalar.activation(out=one[:], in_=zero[:], func=ACT.Exp)
        make_identity(nc, ident_f[:])
        make_identity(nc, ident_b[:])

        for b in range(2):
            nc.sync.dma_start(out=x2_sb[0][:, 1024 * b:1024 * (b + 1)], in_=x2v[:, 0, 1024 * b:1024 * (b + 1)])
        nc.sync.dma_start(out=x1_sb[0][:], in_=x1v[:, 0:1024])
        for b in range(2):
            nc.sync.dma_start(out=x2_sb[1][:, 1024 * b:1024 * (b + 1)], in_=x2v[:, 1, 1024 * b:1024 * (b + 1)])
        for c in range(1, 4):
            nc.sync.dma_start(out=x1_sb[c][:], in_=x1v[:, 1024 * c:1024 * (c + 1)])

        x2_transpose(0, 0, 0)
        x2_transpose(0, 1, 1)
        x1_transpose(0, 2)
        x2_transpose(1, 0, 3)
        x2_transpose(1, 1, 4)
        for c in range(1, 4):
            x1_transpose(c, 4 + c)

        x2_group_keys(0, 0, True)
        x2_group_keys(0, 1, True)
        quantise(x2k_c[0][:], x2k_s[0][:], x2k_g[0][:])
        x2_group(0, 0)
        x2_group(0, 1)
        x1_group(0)
        x2_group(1, 0)
        x2_group(1, 1)
        x1_group(1)
        x1_group(2)
        x1_group(3)
        quantise(x2t_c[0][:], x2t_s[0][:], x2t_g[0][:])
        quantise(x1t_c[0][:], x1t_s[0][:], x1t_g[0][:])
        x2_group_keys(1, 0, True)
        quantise(x2t_c[1][:], x2t_s[1][:], x2t_g[1][:])
        x2_group_keys(1, 1, True)
        quantise(x1t_c[1][:], x1t_s[1][:], x1t_g[1][:])

        for i in range(SCORES_AHEAD):
            scores(i)
            scale_and_maximum(i)
        quantise(x1t_c[2][:], x1t_s[2][:], x1t_g[2][:])
        quantise(x2k_c[1][:], x2k_s[1][:], x2k_g[1][:])
        quantise(x1t_c[3][:], x1t_s[3][:], x1t_g[3][:])

        def in_range(i):
            return 0 <= i < NT

        for n in range(-EXP_AHEAD, NT + QUANT_BEHIND + OUT_BEHIND):
            if in_range(n - QUANT_BEHIND - OUT_BEHIND):
                output(n - QUANT_BEHIND - OUT_BEHIND)
            if in_range(n):
                group_keys(n)
            if in_range(n - QUANT_BEHIND):
                second_matmul(n - QUANT_BEHIND)
            if SCORES_AHEAD <= n + EXP_AHEAD + SCORES_AHEAD < NT:
                scores(n + EXP_AHEAD + SCORES_AHEAD)
                scale_and_maximum(n + EXP_AHEAD + SCORES_AHEAD)
            if in_range(n + EXP_AHEAD):
                exponential(n + EXP_AHEAD)
                keys_to_partitions(n + EXP_AHEAD)
